import numpy as np
import ml_dtypes


def mxq(x, axis, fmt="e4m3"):
    dtype, down = {"e4m3": (ml_dtypes.float8_e4m3fn, 7), "e5m2": (ml_dtypes.float8_e5m2, 14)}[fmt]
    v = np.moveaxis(np.asarray(x, np.float32).astype(ml_dtypes.bfloat16).astype(np.float64), axis, -1)
    blocks = v.reshape(v.shape[:-1] + (-1, 32))
    amax = np.abs(blocks).max(-1, keepdims=True)
    byte = np.maximum(np.where(amax > 0, np.frexp(amax)[1] - 1 + 127, 0) - down, 1)
    scale = np.exp2(byte - 127.0)
    codes = (blocks / scale).astype(np.float32).astype(dtype).astype(np.float64)
    return np.moveaxis((codes * scale).reshape(v.shape), -1, axis)


WIDE = False


def mx_kscale(k):
    if not WIDE:
        return np.ones(k)
    levels = np.array([30, -30])
    if k % 512:
        return np.exp2(np.random.permutation(np.resize(levels, k // 32))).repeat(32)
    a = np.empty((k // 512, 16))
    for p in range(k // 512):
        a[p, :8] = np.random.permutation(np.resize(levels, 8))
        for g in range(8):
            far = levels[np.abs(levels - a[p, g]) >= 10]
            a[p, g + 8] = far[np.random.randint(len(far))]
    return np.exp2(a.ravel()).repeat(32)


BF16 = ml_dtypes.bfloat16


def bf(x):
    return np.asarray(x, np.float32).astype(BF16)


def f64(x):
    return np.asarray(x).astype(np.float64)


B, T, E, H, FF = 4, 1024, 1024, 8, 512
EPS = 1e-5


def layernorm(r, g):
    mu = r.mean(-1, keepdims=True)
    var = ((r - mu) ** 2).mean(-1, keepdims=True)
    return (r - mu) / np.sqrt(var + EPS) * g


def setup_inputs():
    t = mx_kscale(FF)
    z = np.random.standard_normal((B, T, FF))
    return {
        "y_act": bf(z * z / (1.0 + np.exp(-z)) * t),
        "h": bf(np.random.standard_normal((B, T, E))),
        "W2": bf(np.random.standard_normal((FF, E)) / np.sqrt(FF) / t[:, None]),
        "b2": bf(np.random.standard_normal(E) * 0.1),
        "g2": bf(1.0 + np.random.standard_normal(E) * 0.1),
    }


def reference(y_act, h, W2, b2, g2):
    ff = (mxq(f64(y_act), 2, "e5m2") @ mxq(f64(W2), 0, "e5m2")) + f64(b2)
    return layernorm(ff + f64(h), f64(g2))

@@ -1,0 +1,308 @@
+from contextlib import ExitStack
+
+import concourse.mybir as mybir
+from concourse.masks import make_identity
+
+F32 = mybir.dt.float32
+BF16 = mybir.dt.bfloat16
+U32 = mybir.dt.uint32
+U8 = mybir.dt.uint8
+E5X4 = mybir.dt.float8_e5m2_x4
+ALU = mybir.AluOpType
+ACT = mybir.ActivationFunctionType
+
+TOK = 4 * 1024
+FF = 512
+E = 1024
+EPS = 1e-5
+
+P = 128
+NQ = TOK // (2 * P)
+NT = 2 * NQ
+NB = 512
+NH = E // NB
+
+FLOPS = 2 * TOK * FF * E
+
+G_AHEAD = 3
+LOAD_AHEAD = 4
+W_V_COLS = 336
+
+
+def tile_transformerblock_pb_t_kernel(tc, y_act, h, W2, b2, g2, out):
+    nc = tc.nc
+    y_v = y_act.flatten_outer_dims().rearrange("(q p j) k -> q p (j k)", p=P, j=2)
+    h_v = h.flatten_outer_dims().rearrange("(q p j) e -> q p (j e)", p=P, j=2)
+    o_v = out.flatten_outer_dims().rearrange("(q p j) e -> q p j e", p=P, j=2)
+    w_v = W2.rearrange("(p j) n -> p j n", j=4)
+
+    with ExitStack() as ctx:
+        const = ctx.enter_context(tc.tile_pool(name="const", bufs=1))
+        ypool = ctx.enter_context(tc.tile_pool(name="ypool", bufs=NQ))
+        hpool = ctx.enter_context(tc.tile_pool(name="hpool", bufs=NQ))
+        qpool = ctx.enter_context(tc.tile_pool(name="qpool", bufs=3))
+        rpool = ctx.enter_context(tc.tile_pool(name="rpool", bufs=6))
+        tpool = ctx.enter_context(tc.tile_pool(name="tpool", bufs=5))
+        spool = ctx.enter_context(tc.tile_pool(name="spool", bufs=8))
+        ps_g2 = ctx.enter_context(tc.psum_pool(name="ps_g2", bufs=1))
+        ps_acc = ctx.enter_context(tc.psum_pool(name="ps_acc", bufs=2))
+        ps_xt = ctx.enter_context(tc.psum_pool(name="ps_xt", bufs=2))
+        ctx.enter_context(tc.manual_schedule())
+
+        y_t = {}
+        h_t = {}
+        xt = {}
+        ygrp = {}
+        ycodes = {}
+        yscale = {}
+        acc = {}
+        hb = {}
+        sums = {}
+        negmu = {}
+        ssq = {}
+        std = {}
+        rstd = {}
+        tt = {}
+
+        def load_y(q):
+            y_t[q] = ypool.tile([P, 2 * FF], BF16, name="y_t")
+            nc.sync.dma_start(out=y_t[q][:], in_=y_v[q])
+
+        def alloc_h(q):
+            h_t[q] = hpool.tile([P, 2 * E], BF16, name="h_t")
+
+        def load_h(q, lo, hi):
+            nc.sync.dma_start(out=h_t[q][:, lo * E : hi * E], in_=h_v[q][:, lo * E : hi * E])
+
+        def transposes(q):
+            words = y_t[q][:].bitcast(F32)
+            xt[q] = ps_xt.tile([P, 4, P], F32, name="xt")
+            for j in range(2):
+                for u in range(2):
+                    nc.tensor.transpose(
+                        xt[q][:, 2 * j + u, :], words[:, 256 * j + u : 256 * (j + 1) : 2], ident[:]
+                    )
+
+        def copy_y(q):
+            ygrp[q] = qpool.tile([P, 2 * P * 4], BF16, name="ygrp", align_bytes=64)
+            nc.scalar.copy(
+                out=ygrp[q][:].bitcast(F32).rearrange("p (j r u) -> p j r u", j=2, u=2),
+                in_=xt[q][:].rearrange("p (j u) r -> p j r u", j=2, u=2),
+            )
+
+        def quant_y(q):
+            ycodes[q] = qpool.tile([P, 2 * P], U32, name="ycodes", align_bytes=64)
+            yscale[q] = qpool.tile([P, 2 * P], U8, name="yscale", align_bytes=64)
+            nc.vector.quantize_mx(out=ycodes[q][:].bitcast(E5X4), scales=yscale[q][:], in_=ygrp[q][:])
+
+        def mm(i):
+            q, j = divmod(i, 2)
+            cols = slice(j * P, (j + 1) * P)
+            for n in range(NH):
+                acc[(i, n)] = ps_acc.tile([P, NB], F32, name="acc%d" % n)
+                nc.tensor.matmul_mx(
+                    out=acc[(i, n)][:],
+                    lhsT=ycodes[q][:, cols].bitcast(E5X4),
+                    lhsT_scale=yscale[q][:, cols],
+                    rhs=w_codes[:, n * NB : (n + 1) * NB].bitcast(E5X4),
+                    rhs_scale=w_scale[:, n * NB : (n + 1) * NB],
+                    start=True,
+                    stop=True,
+                )
+
+        def p2(i):
+            q, j = divmod(i, 2)
+            hb[i] = rpool.tile([P, E], F32, name="hb")
+            nc.gpsimd.tensor_tensor(out=hb[i][:], in0=h_t[q][:, j * E : (j + 1) * E], in1=b2_sb[:], op=ALU.add)
+
+        def p1(i, n):
+            if n == 0:
+                sums[i] = spool.tile([P, NH], F32, name="sums")
+            half = slice(n * NB, (n + 1) * NB)
+            nc.vector.scalar_tensor_tensor(
+                out=hb[i][:, half],
+                in0=acc[(i, n)][:],
+                scalar=0.0,
+                in1=hb[i][:, half],
+                op0=ALU.add,
+                op1=ALU.add,
+                accum_out=sums[i][:, n : n + 1],
+            )
+
+        def neg_mean(i):
+            negmu[i] = spool.tile([P, 1], F32, name="negmu")
+            nc.vector.tensor_scalar(
+                out=negmu[i][:],
+                in0=sums[i][:, 0:1],
+                scalar1=sums[i][:, 1:2],
+                scalar2=-1.0 / E,
+                op0=ALU.add,
+                op1=ALU.mult,
+            )
+
+        def p3(i):
+            ssq[i] = spool.tile([P, 1], F32, name="ssq")
+            nc.scalar.activation(
+                out=junk[:], in_=hb[i][:], func=ACT.Square, bias=negmu[i][:, 0:1], scale=1.0, accum_out=ssq[i][:]
+            )
+
+        def sqrt(i):
+            std[i] = spool.tile([P, 1], F32, name="std")
+            nc.scalar.activation(out=std[i][:], in_=ssq[i][:], func=ACT.Sqrt, bias=EPS, scale=1.0 / E)
+
+        def recip(i):
+            rstd[i] = spool.tile([P, 1], F32, name="rstd")
+            nc.vector.reciprocal(out=rstd[i][:], in_=std[i][:])
+
+        def p4(i, n):
+            if n == 0:
+                tt[i] = tpool.tile([P, E], F32, name="tt")
+            half = slice(n * NB, (n + 1) * NB)
+            nc.vector.scalar_tensor_tensor(
+                out=tt[i][:, half],
+                in0=hb[i][:, half],
+                scalar=negmu[i][:, 0:1],
+                in1=g2_ps[n][:],
+                op0=ALU.add,
+                op1=ALU.mult,
+            )
+
+        def p5_scalar(i, lo, hi):
+            nc.scalar.activation(out=tt[i][:, lo:hi], in_=tt[i][:, lo:hi], func=ACT.Copy, scale=rstd[i][:, 0:1])
+
+        def p5_gpsimd(i, lo, hi):
+            nc.gpsimd.tensor_scalar(
+                out=tt[i][:, lo:hi],
+                in0=tt[i][:, lo:hi],
+                scalar1=rstd[i][:, 0:1],
+                scalar2=0.0,
+                op0=ALU.mult,
+                op1=ALU.add,
+            )
+
+        def store(i, lo, hi):
+            q, j = divmod(i, 2)
+            nc.sync.dma_start(out=o_v[q][:, j, lo:hi], in_=tt[i][:, lo:hi])
+
+        def p5_store(i):
+            if i == NT - 1:
+                p5_scalar(i, 0, NB)
+                store(i, 0, NB)
+                p5_gpsimd(i, NB, E)
+                store(i, NB, E)
+            elif i >= NT - 3:
+                p5_gpsimd(i, 0, E)
+                store(i, 0, E)
+            else:
+                p5_scalar(i, 0, E)
+                store(i, 0, E)
+
+        rows = const.tile([P, 2 * E], BF16, name="rows")
+        ones = const.tile([P, P], BF16, name="ones")
+        one1 = const.tile([P, 1], F32, name="one1")
+        warm = const.tile([P, 1], F32, name="warm")
+        junk = const.tile([P, E], F32, name="junk")
+        w_raw = const.tile([P, 4, E], BF16, name="w_raw")
+        nc.vector.memset(rows[:], 0.0)
+        nc.vector.memset(ones[:], 1.0)
+        nc.vector.memset(one1[:], 1.0)
+
+        load_y(0)
+        nc.sync.dma_start(out=rows[0:1, 0:E], in_=b2.rearrange("(o e) -> o e", o=1))
+        nc.sync.dma_start(out=rows[0:1, E : 2 * E], in_=g2.rearrange("(o e) -> o e", o=1))
+        nc.sync.dma_start(out=w_raw[:, :, 0:NB], in_=w_v[:, :, 0:NB])
+        alloc_h(0)
+        load_h(0, 0, 1)
+        nc.sync.dma_start(out=w_raw[:, :, NB:E], in_=w_v[:, :, NB:E])
+        load_h(0, 1, 2)
+        for q in range(1, LOAD_AHEAD):
+            load_y(q)
+            alloc_h(q)
+            load_h(q, 0, 2)
+
+        nc.scalar.activation(out=warm[:], in_=one1[:], func=ACT.Sqrt)
+
+        ident = const.tile([P, P], F32, name="ident")
+        make_identity(nc, ident[:])
+
+        transposes(0)
+        copy_y(0)
+
+        b2_sb = const.tile([P, E], BF16, name="b2_sb")
+        g2_ps = []
+        for n in range(NH):
+            b2_ps = ps_acc.tile([P, NB], F32, name="acc%d" % n)
+            nc.tensor.matmul(out=b2_ps[:], lhsT=ones[:], rhs=rows[:, n * NB : (n + 1) * NB], start=True, stop=True)
+            nc.scalar.copy(out=b2_sb[:, n * NB : (n + 1) * NB], in_=b2_ps[:])
+        for n in range(NH):
+            g2_ps.append(ps_g2.tile([P, NB], F32, name="g2_ps%d" % n))
+            nc.tensor.matmul(
+                out=g2_ps[n][:], lhsT=ones[:], rhs=rows[:, E + n * NB : E + (n + 1) * NB], start=True, stop=True
+            )
+
+        w_grp = const.tile([P, E, 4], BF16, name="w_grp", align_bytes=64)
+        w_codes = const.tile([P, E], U32, name="w_codes", align_bytes=64)
+        w_scale = const.tile([P, E], U8, name="w_scale", align_bytes=64)
+
+        def w_views(lo, hi):
+            return w_grp[:, lo:hi, :], w_raw[:, :, lo:hi].rearrange("p j w -> p w j")
+
+        def w_quant(n):
+            nc.vector.quantize_mx(
+                out=w_codes[:, n * NB : (n + 1) * NB].bitcast(E5X4),
+                scales=w_scale[:, n * NB : (n + 1) * NB],
+                in_=w_grp[:, n * NB : (n + 1) * NB, :].rearrange("p w j -> p (w j)"),
+            )
+
+        dst, src = w_views(0, NB)
+        nc.vector.tensor_copy(out=dst, in_=src)
+        quant_y(0)
+        dst, src = w_views(NB, NB + W_V_COLS)
+        nc.vector.tensor_copy(out=dst, in_=src)
+        dst, src = w_views(NB + W_V_COLS, E)
+        nc.scalar.copy(out=dst, in_=src)
+        w_quant(0)
+        w_quant(1)
+
+        transposes(1)
+        copy_y(1)
+
+        for i in range(G_AHEAD):
+            p2(i)
+        mm(0)
+
+        for i in range(NT + 3):
+            q = i // 2
+            even = i % 2 == 0
+            if even and q + LOAD_AHEAD < NQ:
+                load_y(q + LOAD_AHEAD)
+                alloc_h(q + LOAD_AHEAD)
+                load_h(q + LOAD_AHEAD, 0, 2)
+            if i + G_AHEAD < NT:
+                p2(i + G_AHEAD)
+            if i + 1 < NT:
+                mm(i + 1)
+            if even and q + 2 < NQ:
+                transposes(q + 2)
+            if i < NT:
+                p1(i, 0)
+            if 0 <= i - 2 < NT:
+                recip(i - 2)
+            if i < NT:
+                p1(i, 1)
+            if 0 <= i - 1 < NT:
+                p4(i - 1, 0)
+            if i < NT:
+                neg_mean(i)
+            if 0 <= i - 1 < NT:
+                p4(i - 1, 1)
+            if even and q + 1 < NQ:
+                quant_y(q + 1)
+            if 0 <= i - 1 < NT:
+                p3(i - 1)
+            if 0 <= i - 2 < NT:
+                p5_store(i - 2)
+            if 0 <= i - 1 < NT:
+                sqrt(i - 1)
+            if (not even) and q + 2 < NQ:
+                copy_y(q + 2)

@@ -25,8 +25,11 @@ NH = E // NB
 FLOPS = 2 * TOK * FF * E
 
 G_AHEAD = 3
-LOAD_AHEAD = 4
+H_AHEAD = 4
+Y_AHEAD = 8
 W_V_COLS = 336
+PE_HB = 2
+BATCHES = ((0, 2), (2, 2), (4, 4), (8, 4), (12, 4))
 
 
 def tile_transformerblock_pb_t_kernel(tc, y_act, h, W2, b2, g2, out):
@@ -40,7 +43,7 @@ def tile_transformerblock_pb_t_kernel(tc, y_act, h, W2, b2, g2, out):
         const = ctx.enter_context(tc.tile_pool(name="const", bufs=1))
         ypool = ctx.enter_context(tc.tile_pool(name="ypool", bufs=NQ))
         hpool = ctx.enter_context(tc.tile_pool(name="hpool", bufs=NQ))
-        qpool = ctx.enter_context(tc.tile_pool(name="qpool", bufs=3))
+        qpool = ctx.enter_context(tc.tile_pool(name="qpool", bufs=2))
         rpool = ctx.enter_context(tc.tile_pool(name="rpool", bufs=6))
         tpool = ctx.enter_context(tc.tile_pool(name="tpool", bufs=5))
         spool = ctx.enter_context(tc.tile_pool(name="spool", bufs=8))
@@ -64,6 +67,21 @@ def tile_transformerblock_pb_t_kernel(tc, y_act, h, W2, b2, g2, out):
         rstd = {}
         tt = {}
 
+        batch_of = {}
+        quant_tick = {}
+        prep_tick = {}
+        last_tick = 0
+        for b, (q0, n) in enumerate(BATCHES):
+            for q in range(q0, q0 + n):
+                batch_of[q] = (b, q - q0)
+            if b > 0:
+                tick = 2 * q0 - 2
+                quant_tick[tick] = b
+                step = max(1, (tick - last_tick) // n)
+                for q in range(q0, q0 + n):
+                    prep_tick[tick - 1 - step * (q0 + n - 1 - q)] = q
+                last_tick = tick
+
         def load_y(q):
             y_t[q] = ypool.tile([P, 2 * FF], BF16, name="y_t")
             nc.sync.dma_start(out=y_t[q][:], in_=y_v[q])
@@ -84,20 +102,24 @@ def tile_transformerblock_pb_t_kernel(tc, y_act, h, W2, b2, g2, out):
                     )
 
         def copy_y(q):
-            ygrp[q] = qpool.tile([P, 2 * P * 4], BF16, name="ygrp", align_bytes=64)
+            b, k = batch_of[q]
+            if k == 0:
+                ygrp[b] = qpool.tile([P, BATCHES[b][1] * 2 * P * 4], BF16, name="ygrp", align_bytes=64)
             nc.scalar.copy(
-                out=ygrp[q][:].bitcast(F32).rearrange("p (j r u) -> p j r u", j=2, u=2),
+                out=ygrp[b][:, k * 1024 : (k + 1) * 1024].bitcast(F32).rearrange("p (j r u) -> p j r u", j=2, u=2),
                 in_=xt[q][:].rearrange("p (j u) r -> p j r u", j=2, u=2),
             )
 
-        def quant_y(q):
-            ycodes[q] = qpool.tile([P, 2 * P], U32, name="ycodes", align_bytes=64)
-            yscale[q] = qpool.tile([P, 2 * P], U8, name="yscale", align_bytes=64)
-            nc.vector.quantize_mx(out=ycodes[q][:].bitcast(E5X4), scales=yscale[q][:], in_=ygrp[q][:])
+        def quant_y(b):
+            width = BATCHES[b][1] * 2 * P
+            ycodes[b] = qpool.tile([P, width], U32, name="ycodes", align_bytes=64)
+            yscale[b] = qpool.tile([P, width], U8, name="yscale", align_bytes=64)
+            nc.vector.quantize_mx(out=ycodes[b][:].bitcast(E5X4), scales=yscale[b][:], in_=ygrp[b][:])
 
         def mm(i):
             q, j = divmod(i, 2)
-            cols = slice(j * P, (j + 1) * P)
+            q, k = batch_of[q]
+            cols = slice((2 * k + j) * P, (2 * k + j + 1) * P)
             for n in range(NH):
                 acc[(i, n)] = ps_acc.tile([P, NB], F32, name="acc%d" % n)
                 nc.tensor.matmul_mx(
@@ -208,6 +230,7 @@ def tile_transformerblock_pb_t_kernel(tc, y_act, h, W2, b2, g2, out):
         nc.vector.memset(one1[:], 1.0)
 
         load_y(0)
+        load_y(1)
         nc.sync.dma_start(out=rows[0:1, 0:E], in_=b2.rearrange("(o e) -> o e", o=1))
         nc.sync.dma_start(out=rows[0:1, E : 2 * E], in_=g2.rearrange("(o e) -> o e", o=1))
         nc.sync.dma_start(out=w_raw[:, :, 0:NB], in_=w_v[:, :, 0:NB])
@@ -215,8 +238,9 @@ def tile_transformerblock_pb_t_kernel(tc, y_act, h, W2, b2, g2, out):
         load_h(0, 0, 1)
         nc.sync.dma_start(out=w_raw[:, :, NB:E], in_=w_v[:, :, NB:E])
         load_h(0, 1, 2)
-        for q in range(1, LOAD_AHEAD):
-            load_y(q)
+        for q in range(1, H_AHEAD):
+            load_y(2 * q)
+            load_y(2 * q + 1)
             alloc_h(q)
             load_h(q, 0, 2)
 
@@ -224,9 +248,13 @@ def tile_transformerblock_pb_t_kernel(tc, y_act, h, W2, b2, g2, out):
 
         ident = const.tile([P, P], F32, name="ident")
         make_identity(nc, ident[:])
+        ident_bf = const.tile([P, P], BF16, name="ident_bf")
+        make_identity(nc, ident_bf[:])
 
         transposes(0)
         copy_y(0)
+        transposes(1)
+        copy_y(1)
 
         b2_sb = const.tile([P, E], BF16, name="b2_sb")
         g2_ps = []
@@ -264,26 +292,40 @@ def tile_transformerblock_pb_t_kernel(tc, y_act, h, W2, b2, g2, out):
         w_quant(0)
         w_quant(1)
 
-        transposes(1)
-        copy_y(1)
+        for i in range(PE_HB):
+            hb[i] = rpool.tile([P, E], F32, name="hb")
+            for n in range(NH):
+                hb_ps = ps_acc.tile([P, NB], F32, name="acc%d" % n)
+                nc.tensor.matmul(
+                    out=hb_ps[:],
+                    lhsT=ident_bf[:],
+                    rhs=h_t[0][:, i * E + n * NB : i * E + (n + 1) * NB],
+                    start=True,
+                    stop=False,
+                )
+                nc.tensor.matmul(
+                    out=hb_ps[:], lhsT=ones[:], rhs=rows[:, n * NB : (n + 1) * NB], start=False, stop=True
+                )
+                nc.scalar.copy(out=hb[i][:, n * NB : (n + 1) * NB], in_=hb_ps[:])
 
-        for i in range(G_AHEAD):
+        for i in range(PE_HB, G_AHEAD):
             p2(i)
         mm(0)
 
         for i in range(NT + 3):
             q = i // 2
             even = i % 2 == 0
-            if even and q + LOAD_AHEAD < NQ:
-                load_y(q + LOAD_AHEAD)
-                alloc_h(q + LOAD_AHEAD)
-                load_h(q + LOAD_AHEAD, 0, 2)
+            if even and q + H_AHEAD < NQ:
+                alloc_h(q + H_AHEAD)
+                load_h(q + H_AHEAD, 0, 2)
+            if even and q + Y_AHEAD < NQ:
+                load_y(q + Y_AHEAD)
             if i + G_AHEAD < NT:
                 p2(i + G_AHEAD)
             if i + 1 < NT:
                 mm(i + 1)
-            if even and q + 2 < NQ:
-                transposes(q + 2)
+            if i in prep_tick:
+                transposes(prep_tick[i])
             if i < NT:
                 p1(i, 0)
             if 0 <= i - 2 < NT:
@@ -296,13 +338,13 @@ def tile_transformerblock_pb_t_kernel(tc, y_act, h, W2, b2, g2, out):
                 neg_mean(i)
             if 0 <= i - 1 < NT:
                 p4(i - 1, 1)
-            if even and q + 1 < NQ:
-                quant_y(q + 1)
+            if i in quant_tick:
+                quant_y(quant_tick[i])
             if 0 <= i - 1 < NT:
                 p3(i - 1)
             if 0 <= i - 2 < NT:
                 p5_store(i - 2)
             if 0 <= i - 1 < NT:
                 sqrt(i - 1)
-            if (not even) and q + 2 < NQ:
-                copy_y(q + 2)
+            if i in prep_tick:
+                copy_y(prep_tick[i])

@@ -28,7 +28,8 @@ G_AHEAD = 3
 H_AHEAD = 4
 Y_AHEAD = 8
 W_V_COLS = 336
-PE_HB = 2
+PE_HEAD = (0, 1)
+PE_TICK = {0: 2, 12: 15, 20: 23}
 BATCHES = ((0, 2), (2, 2), (4, 4), (8, 4), (12, 4))
 
 
@@ -136,6 +137,23 @@ def tile_transformerblock_pb_t_kernel(tc, y_act, h, W2, b2, g2, out):
             q, j = divmod(i, 2)
             hb[i] = rpool.tile([P, E], F32, name="hb")
             nc.gpsimd.tensor_tensor(out=hb[i][:], in0=h_t[q][:, j * E : (j + 1) * E], in1=b2_sb[:], op=ALU.add)
+
+        def pe_hb(i, pool, names, copiers):
+            q, j = divmod(i, 2)
+            hb[i] = rpool.tile([P, E], F32, name="hb")
+            for n in range(NH):
+                hb_ps = pool.tile([P, NB], F32, name=names[n])
+                nc.tensor.matmul(
+                    out=hb_ps[:],
+                    lhsT=ident_bf[:],
+                    rhs=h_t[q][:, j * E + n * NB : j * E + (n + 1) * NB],
+                    start=True,
+                    stop=False,
+                )
+                nc.tensor.matmul(
+                    out=hb_ps[:], lhsT=ones[:], rhs=rows[:, n * NB : (n + 1) * NB], start=False, stop=True
+                )
+                copiers[n](out=hb[i][:, n * NB : (n + 1) * NB], in_=hb_ps[:])
 
         def p1(i, n):
             if n == 0:
@@ -256,7 +274,7 @@ def tile_transformerblock_pb_t_kernel(tc, y_act, h, W2, b2, g2, out):
         transposes(1)
         copy_y(1)
 
-        b2_sb = const.tile([P, E], BF16, name="b2_sb")
+        b2_sb = const.tile([P, E], F32, name="b2_sb")
         g2_ps = []
         for n in range(NH):
             b2_ps = ps_acc.tile([P, NB], F32, name="acc%d" % n)
@@ -292,25 +310,10 @@ def tile_transformerblock_pb_t_kernel(tc, y_act, h, W2, b2, g2, out):
         w_quant(0)
         w_quant(1)
 
-        for i in range(PE_HB):
-            hb[i] = rpool.tile([P, E], F32, name="hb")
-            for n in range(NH):
-                hb_ps = ps_acc.tile([P, NB], F32, name="acc%d" % n)
-                nc.tensor.matmul(
-                    out=hb_ps[:],
-                    lhsT=ident_bf[:],
-                    rhs=h_t[0][:, i * E + n * NB : i * E + (n + 1) * NB],
-                    start=True,
-                    stop=False,
-                )
-                nc.tensor.matmul(
-                    out=hb_ps[:], lhsT=ones[:], rhs=rows[:, n * NB : (n + 1) * NB], start=False, stop=True
-                )
-                nc.scalar.copy(out=hb[i][:, n * NB : (n + 1) * NB], in_=hb_ps[:])
-
-        for i in range(PE_HB, G_AHEAD):
-            p2(i)
+        for i in PE_HEAD:
+            pe_hb(i, ps_acc, ("acc0", "acc1"), (nc.scalar.copy, nc.scalar.copy))
         mm(0)
+        pe_tiles = list(PE_HEAD) + [PE_TICK[t] for t in PE_TICK]
 
         for i in range(NT + 3):
             q = i // 2
@@ -320,7 +323,7 @@ def tile_transformerblock_pb_t_kernel(tc, y_act, h, W2, b2, g2, out):
                 load_h(q + H_AHEAD, 0, 2)
             if even and q + Y_AHEAD < NQ:
                 load_y(q + Y_AHEAD)
-            if i + G_AHEAD < NT:
+            if i + G_AHEAD < NT and i + G_AHEAD not in pe_tiles:
                 p2(i + G_AHEAD)
             if i + 1 < NT:
                 mm(i + 1)
@@ -348,3 +351,10 @@ def tile_transformerblock_pb_t_kernel(tc, y_act, h, W2, b2, g2, out):
                 sqrt(i - 1)
             if i in prep_tick:
                 copy_y(prep_tick[i])
+            if i in PE_TICK:
+                pe_hb(
+                    PE_TICK[i],
+                    ps_xt,
+                    ("xt", "xt"),
+                    (nc.scalar.copy if i == 0 else nc.vector.tensor_copy, nc.scalar.copy),
+                )

@@ -64,7 +64,6 @@ def tile_transformerblock_pb_t_kernel(tc, y_act, h, W2, b2, g2, out):
         sums = {}
         negmu = {}
         ssq = {}
-        std = {}
         rstd = {}
         tt = {}
 
@@ -186,13 +185,11 @@ def tile_transformerblock_pb_t_kernel(tc, y_act, h, W2, b2, g2, out):
                 out=junk[:], in_=hb[i][:], func=ACT.Square, bias=negmu[i][:, 0:1], scale=1.0, accum_out=ssq[i][:]
             )
 
-        def sqrt(i):
-            std[i] = spool.tile([P, 1], F32, name="std")
-            nc.scalar.activation(out=std[i][:], in_=ssq[i][:], func=ACT.Sqrt, bias=EPS, scale=1.0 / E)
-
-        def recip(i):
+        def rsqrt(i):
             rstd[i] = spool.tile([P, 1], F32, name="rstd")
-            nc.vector.reciprocal(out=rstd[i][:], in_=std[i][:])
+            nc.scalar.activation(
+                out=rstd[i][:], in_=ssq[i][:], func=ACT.Abs_reciprocal_sqrt, bias=EPS, scale=1.0 / E
+            )
 
         def p4(i, n):
             if n == 0:
@@ -220,6 +217,16 @@ def tile_transformerblock_pb_t_kernel(tc, y_act, h, W2, b2, g2, out):
                 op1=ALU.add,
             )
 
+        def p5_vector(i, lo, hi):
+            nc.vector.tensor_scalar(
+                out=tt[i][:, lo:hi],
+                in0=tt[i][:, lo:hi],
+                scalar1=rstd[i][:, 0:1],
+                scalar2=0.0,
+                op0=ALU.mult,
+                op1=ALU.add,
+            )
+
         def store(i, lo, hi):
             q, j = divmod(i, 2)
             nc.sync.dma_start(out=o_v[q][:, j, lo:hi], in_=tt[i][:, lo:hi])
@@ -228,7 +235,7 @@ def tile_transformerblock_pb_t_kernel(tc, y_act, h, W2, b2, g2, out):
             if i == NT - 1:
                 p5_scalar(i, 0, NB)
                 store(i, 0, NB)
-                p5_gpsimd(i, NB, E)
+                p5_vector(i, NB, E)
                 store(i, NB, E)
             elif i >= NT - 3:
                 p5_gpsimd(i, 0, E)
@@ -262,7 +269,7 @@ def tile_transformerblock_pb_t_kernel(tc, y_act, h, W2, b2, g2, out):
             alloc_h(q)
             load_h(q, 0, 2)
 
-        nc.scalar.activation(out=warm[:], in_=one1[:], func=ACT.Sqrt)
+        nc.scalar.activation(out=warm[:], in_=one1[:], func=ACT.Abs_reciprocal_sqrt)
 
         ident = const.tile([P, P], F32, name="ident")
         make_identity(nc, ident[:])
@@ -331,8 +338,6 @@ def tile_transformerblock_pb_t_kernel(tc, y_act, h, W2, b2, g2, out):
                 transposes(prep_tick[i])
             if i < NT:
                 p1(i, 0)
-            if 0 <= i - 2 < NT:
-                recip(i - 2)
             if i < NT:
                 p1(i, 1)
             if 0 <= i - 1 < NT:
@@ -348,7 +353,7 @@ def tile_transformerblock_pb_t_kernel(tc, y_act, h, W2, b2, g2, out):
             if 0 <= i - 2 < NT:
                 p5_store(i - 2)
             if 0 <= i - 1 < NT:
-                sqrt(i - 1)
+                rsqrt(i - 1)
             if i in prep_tick:
                 copy_y(prep_tick[i])
             if i in PE_TICK:
@@ -356,5 +361,5 @@ def tile_transformerblock_pb_t_kernel(tc, y_act, h, W2, b2, g2, out):
                     PE_TICK[i],
                     ps_xt,
                     ("xt", "xt"),
-                    (nc.scalar.copy if i == 0 else nc.vector.tensor_copy, nc.scalar.copy),
+                    (nc.vector.tensor_copy, nc.vector.tensor_copy if i == 0 else nc.scalar.copy),
                 )

@@ -191,15 +191,13 @@ def tile_transformerblock_pb_t_kernel(tc, y_act, h, W2, b2, g2, out):
                 out=rstd[i][:], in_=ssq[i][:], func=ACT.Abs_reciprocal_sqrt, bias=EPS, scale=1.0 / E
             )
 
-        def p4(i, n):
-            if n == 0:
-                tt[i] = tpool.tile([P, E], F32, name="tt")
-            half = slice(n * NB, (n + 1) * NB)
+        def p4(i):
+            tt[i] = tpool.tile([P, E], F32, name="tt")
             nc.vector.scalar_tensor_tensor(
-                out=tt[i][:, half],
-                in0=hb[i][:, half],
+                out=tt[i][:],
+                in0=hb[i][:],
                 scalar=negmu[i][:, 0:1],
-                in1=g2_ps[n][:],
+                in1=g2_ps[:],
                 op0=ALU.add,
                 op1=ALU.mult,
             )
@@ -282,15 +280,18 @@ def tile_transformerblock_pb_t_kernel(tc, y_act, h, W2, b2, g2, out):
         copy_y(1)
 
         b2_sb = const.tile([P, E], F32, name="b2_sb")
-        g2_ps = []
         for n in range(NH):
             b2_ps = ps_acc.tile([P, NB], F32, name="acc%d" % n)
             nc.tensor.matmul(out=b2_ps[:], lhsT=ones[:], rhs=rows[:, n * NB : (n + 1) * NB], start=True, stop=True)
             nc.scalar.copy(out=b2_sb[:, n * NB : (n + 1) * NB], in_=b2_ps[:])
+        g2_ps = ps_g2.tile([P, E], BF16, name="g2_ps")
         for n in range(NH):
-            g2_ps.append(ps_g2.tile([P, NB], F32, name="g2_ps%d" % n))
             nc.tensor.matmul(
-                out=g2_ps[n][:], lhsT=ones[:], rhs=rows[:, E + n * NB : E + (n + 1) * NB], start=True, stop=True
+                out=g2_ps[:, n * NB : (n + 1) * NB],
+                lhsT=ones[:],
+                rhs=rows[:, E + n * NB : E + (n + 1) * NB],
+                start=True,
+                stop=True,
             )
 
         w_grp = const.tile([P, E, 4], BF16, name="w_grp", align_bytes=64)
@@ -341,11 +342,9 @@ def tile_transformerblock_pb_t_kernel(tc, y_act, h, W2, b2, g2, out):
             if i < NT:
                 p1(i, 1)
             if 0 <= i - 1 < NT:
-                p4(i - 1, 0)
+                p4(i - 1)
             if i < NT:
                 neg_mean(i)
-            if 0 <= i - 1 < NT:
-                p4(i - 1, 1)
             if i in quant_tick:
                 quant_y(quant_tick[i])
             if 0 <= i - 1 < NT:

@@ -66,6 +66,7 @@ def tile_transformerblock_pb_t_kernel(tc, y_act, h, W2, b2, g2, out):
         ssq = {}
         rstd = {}
         tt = {}
+        hb_ps = {}
 
         batch_of = {}
         quant_tick = {}
@@ -137,22 +138,29 @@ def tile_transformerblock_pb_t_kernel(tc, y_act, h, W2, b2, g2, out):
             hb[i] = rpool.tile([P, E], F32, name="hb")
             nc.gpsimd.tensor_tensor(out=hb[i][:], in0=h_t[q][:, j * E : (j + 1) * E], in1=b2_sb[:], op=ALU.add)
 
-        def pe_hb(i, pool, names, copiers):
+        def pe_mm(i, pool, names):
             q, j = divmod(i, 2)
-            hb[i] = rpool.tile([P, E], F32, name="hb")
             for n in range(NH):
-                hb_ps = pool.tile([P, NB], F32, name=names[n])
+                hb_ps[(i, n)] = pool.tile([P, NB], F32, name=names[n])
                 nc.tensor.matmul(
-                    out=hb_ps[:],
+                    out=hb_ps[(i, n)][:],
                     lhsT=ident_bf[:],
                     rhs=h_t[q][:, j * E + n * NB : j * E + (n + 1) * NB],
                     start=True,
                     stop=False,
                 )
                 nc.tensor.matmul(
-                    out=hb_ps[:], lhsT=ones[:], rhs=rows[:, n * NB : (n + 1) * NB], start=False, stop=True
+                    out=hb_ps[(i, n)][:], lhsT=ones[:], rhs=rows[:, n * NB : (n + 1) * NB], start=False, stop=True
                 )
-                copiers[n](out=hb[i][:, n * NB : (n + 1) * NB], in_=hb_ps[:])
+
+        def pe_copy(i, copiers):
+            hb[i] = rpool.tile([P, E], F32, name="hb")
+            for n in range(NH):
+                copiers[n](out=hb[i][:, n * NB : (n + 1) * NB], in_=hb_ps[(i, n)][:])
+
+        def pe_hb(i, pool, names, copiers):
+            pe_mm(i, pool, names)
+            pe_copy(i, copiers)
 
         def p1(i, n):
             if n == 0:
@@ -333,6 +341,8 @@ def tile_transformerblock_pb_t_kernel(tc, y_act, h, W2, b2, g2, out):
                 load_y(q + Y_AHEAD)
             if i + G_AHEAD < NT and i + G_AHEAD not in pe_tiles:
                 p2(i + G_AHEAD)
+            if i in PE_TICK:
+                pe_mm(PE_TICK[i], ps_xt, ("xt", "xt"))
             if i + 1 < NT:
                 mm(i + 1)
             if i in prep_tick:
@@ -356,9 +366,4 @@ def tile_transformerblock_pb_t_kernel(tc, y_act, h, W2, b2, g2, out):
             if i in prep_tick:
                 copy_y(prep_tick[i])
             if i in PE_TICK:
-                pe_hb(
-                    PE_TICK[i],
-                    ps_xt,
-                    ("xt", "xt"),
-                    (nc.vector.tensor_copy, nc.vector.tensor_copy if i == 0 else nc.scalar.copy),
-                )
+                pe_copy(PE_TICK[i], (nc.vector.tensor_copy, nc.vector.tensor_copy if i == 0 else nc.scalar.copy))

@@ -45,8 +45,8 @@ def tile_transformerblock_pb_t_kernel(tc, y_act, h, W2, b2, g2, out):
         ypool = ctx.enter_context(tc.tile_pool(name="ypool", bufs=NQ))
         hpool = ctx.enter_context(tc.tile_pool(name="hpool", bufs=NQ))
         qpool = ctx.enter_context(tc.tile_pool(name="qpool", bufs=2))
-        rpool = ctx.enter_context(tc.tile_pool(name="rpool", bufs=6))
-        tpool = ctx.enter_context(tc.tile_pool(name="tpool", bufs=5))
+        rpool = ctx.enter_context(tc.tile_pool(name="rpool", bufs=5))
+        tpool = ctx.enter_context(tc.tile_pool(name="tpool", bufs=4))
         spool = ctx.enter_context(tc.tile_pool(name="spool", bufs=8))
         ps_g2 = ctx.enter_context(tc.psum_pool(name="ps_g2", bufs=1))
         ps_acc = ctx.enter_context(tc.psum_pool(name="ps_acc", bufs=2))

@@ -29,7 +29,7 @@ H_AHEAD = 4
 Y_AHEAD = 8
 W_V_COLS = 336
 PE_HEAD = (0, 1)
-PE_TICK = {0: 2, 12: 15, 20: 23}
+PE_TICK = {0: 2, 6: 9, 22: 25}
 BATCHES = ((0, 2), (2, 2), (4, 4), (8, 4), (12, 4))
 
 

@@ -243,6 +243,11 @@ def tile_transformerblock_pb_t_kernel(tc, y_act, h, W2, b2, g2, out):
                 store(i, 0, NB)
                 p5_vector(i, NB, E)
                 store(i, NB, E)
+            elif i == NT - 2:
+                p5_gpsimd(i, 0, NB)
+                store(i, 0, NB)
+                p5_scalar(i, NB, E)
+                store(i, NB, E)
             elif i >= NT - 3:
                 p5_gpsimd(i, 0, E)
                 store(i, 0, E)
@@ -351,9 +356,11 @@ def tile_transformerblock_pb_t_kernel(tc, y_act, h, W2, b2, g2, out):
                 p1(i, 0)
             if i < NT:
                 p1(i, 1)
+            if i == NT - 1:
+                neg_mean(i)
             if 0 <= i - 1 < NT:
                 p4(i - 1)
-            if i < NT:
+            if i < NT - 1:
                 neg_mean(i)
             if i in quant_tick:
                 quant_y(quant_tick[i])

@@ -21,6 +21,7 @@ NQ = TOK // (2 * P)
 NT = 2 * NQ
 NB = 512
 NH = E // NB
+NC = E // P
 
 FLOPS = 2 * TOK * FF * E
 
@@ -29,7 +30,7 @@ H_AHEAD = 4
 Y_AHEAD = 8
 W_V_COLS = 336
 PE_HEAD = (0, 1)
-PE_TICK = {0: 2, 6: 9, 22: 25}
+PE_TICK = {0: 2, 6: 9, 14: 17, 22: 25}
 BATCHES = ((0, 2), (2, 2), (4, 4), (8, 4), (12, 4))
 
 
@@ -50,7 +51,7 @@ def tile_transformerblock_pb_t_kernel(tc, y_act, h, W2, b2, g2, out):
         spool = ctx.enter_context(tc.tile_pool(name="spool", bufs=8))
         ps_g2 = ctx.enter_context(tc.psum_pool(name="ps_g2", bufs=1))
         ps_acc = ctx.enter_context(tc.psum_pool(name="ps_acc", bufs=2))
-        ps_xt = ctx.enter_context(tc.psum_pool(name="ps_xt", bufs=2))
+        ps_xt = ctx.enter_context(tc.psum_pool(name="ps_xt", bufs=3))
         ctx.enter_context(tc.manual_schedule())
 
         y_t = {}
@@ -151,6 +152,28 @@ def tile_transformerblock_pb_t_kernel(tc, y_act, h, W2, b2, g2, out):
                 )
                 nc.tensor.matmul(
                     out=hb_ps[(i, n)][:], lhsT=ones[:], rhs=rows[:, n * NB : (n + 1) * NB], start=False, stop=True
+                )
+
+        def pe_mm_cols(i):
+            q, j = divmod(i, 2)
+            for n in range(NH):
+                hb_ps[(i, n)] = ps_xt.tile([P, NB], F32, name="xt")
+                for c in range(4):
+                    col = 4 * n + c
+                    nc.tensor.matmul(
+                        out=hb_ps[(i, n)][:, c * P : (c + 1) * P],
+                        lhsT=b2c[:, col : col + 1].to_broadcast([P, P]),
+                        rhs=ident[:],
+                        is_transpose=True,
+                        start=c == 0,
+                        stop=False,
+                    )
+                nc.tensor.matmul(
+                    out=hb_ps[(i, n)][:],
+                    lhsT=ident_bf[:],
+                    rhs=h_t[q][:, j * E + n * NB : j * E + (n + 1) * NB],
+                    start=False,
+                    stop=True,
                 )
 
         def pe_copy(i, copiers):
@@ -257,12 +280,14 @@ def tile_transformerblock_pb_t_kernel(tc, y_act, h, W2, b2, g2, out):
 
         rows = const.tile([P, 2 * E], BF16, name="rows")
         ones = const.tile([P, P], BF16, name="ones")
+        vec = const.tile([P, P], BF16, name="vec")
         one1 = const.tile([P, 1], F32, name="one1")
         warm = const.tile([P, 1], F32, name="warm")
         junk = const.tile([P, E], F32, name="junk")
         w_raw = const.tile([P, 4, E], BF16, name="w_raw")
         nc.vector.memset(rows[:], 0.0)
         nc.vector.memset(ones[:], 1.0)
+        nc.vector.memset(vec[:], 0.0)
         nc.vector.memset(one1[:], 1.0)
 
         load_y(0)
@@ -274,6 +299,7 @@ def tile_transformerblock_pb_t_kernel(tc, y_act, h, W2, b2, g2, out):
         load_h(0, 0, 1)
         nc.sync.dma_start(out=w_raw[:, :, NB:E], in_=w_v[:, :, NB:E])
         load_h(0, 1, 2)
+        nc.sync.dma_start(out=vec[0:NC, :], in_=b2.rearrange("(c e) -> c e", c=NC))
         for q in range(1, H_AHEAD):
             load_y(2 * q)
             load_y(2 * q + 1)
@@ -334,6 +360,10 @@ def tile_transformerblock_pb_t_kernel(tc, y_act, h, W2, b2, g2, out):
         for i in PE_HEAD:
             pe_hb(i, ps_acc, ("acc0", "acc1"), (nc.scalar.copy, nc.scalar.copy))
         mm(0)
+        v_ps = ps_xt.tile([P, P], BF16, name="xt")
+        nc.tensor.transpose(v_ps[:], vec[:], ident_bf[:])
+        b2c = const.tile([P, NC], F32, name="b2c")
+        nc.scalar.copy(out=b2c[:], in_=v_ps[:, 0:NC])
         pe_tiles = list(PE_HEAD) + [PE_TICK[t] for t in PE_TICK]
 
         for i in range(NT + 3):
@@ -346,12 +376,14 @@ def tile_transformerblock_pb_t_kernel(tc, y_act, h, W2, b2, g2, out):
                 load_y(q + Y_AHEAD)
             if i + G_AHEAD < NT and i + G_AHEAD not in pe_tiles:
                 p2(i + G_AHEAD)
-            if i in PE_TICK:
-                pe_mm(PE_TICK[i], ps_xt, ("xt", "xt"))
+            if i == 0:
+                pe_mm(PE_TICK[0], ps_xt, ("xt", "xt"))
             if i + 1 < NT:
                 mm(i + 1)
             if i in prep_tick:
                 transposes(prep_tick[i])
+            if i + 1 in PE_TICK:
+                pe_mm_cols(PE_TICK[i + 1])
             if i < NT:
                 p1(i, 0)
             if i < NT:

from contextlib import ExitStack

import concourse.mybir as mybir
from concourse.masks import make_identity

F32 = mybir.dt.float32
BF16 = mybir.dt.bfloat16
U32 = mybir.dt.uint32
U8 = mybir.dt.uint8
E5X4 = mybir.dt.float8_e5m2_x4
ALU = mybir.AluOpType
ACT = mybir.ActivationFunctionType

TOK = 4 * 1024
FF = 512
E = 1024
EPS = 1e-5

P = 128
NQ = TOK // (2 * P)
NT = 2 * NQ
NB = 512
NH = E // NB
NC = E // P

FLOPS = 2 * TOK * FF * E

G_AHEAD = 3
H_AHEAD = 4
Y_AHEAD = 8
W_V_COLS = 336
PE_HEAD = (0, 1)
PE_TICK = {0: 2, 6: 9, 14: 17, 22: 25}
BATCHES = ((0, 2), (2, 2), (4, 4), (8, 4), (12, 4))


def tile_transformerblock_pb_t_kernel(tc, y_act, h, W2, b2, g2, out):
    nc = tc.nc
    y_v = y_act.flatten_outer_dims().rearrange("(q p j) k -> q p (j k)", p=P, j=2)
    h_v = h.flatten_outer_dims().rearrange("(q p j) e -> q p (j e)", p=P, j=2)
    o_v = out.flatten_outer_dims().rearrange("(q p j) e -> q p j e", p=P, j=2)
    w_v = W2.rearrange("(p j) n -> p j n", j=4)

    with ExitStack() as ctx:
        const = ctx.enter_context(tc.tile_pool(name="const", bufs=1))
        ypool = ctx.enter_context(tc.tile_pool(name="ypool", bufs=NQ))
        hpool = ctx.enter_context(tc.tile_pool(name="hpool", bufs=NQ))
        qpool = ctx.enter_context(tc.tile_pool(name="qpool", bufs=2))
        rpool = ctx.enter_context(tc.tile_pool(name="rpool", bufs=5))
        tpool = ctx.enter_context(tc.tile_pool(name="tpool", bufs=4))
        spool = ctx.enter_context(tc.tile_pool(name="spool", bufs=8))
        ps_g2 = ctx.enter_context(tc.psum_pool(name="ps_g2", bufs=1))
        ps_acc = ctx.enter_context(tc.psum_pool(name="ps_acc", bufs=2))
        ps_xt = ctx.enter_context(tc.psum_pool(name="ps_xt", bufs=3))
        ctx.enter_context(tc.manual_schedule())

        y_t = {}
        h_t = {}
        xt = {}
        ygrp = {}
        ycodes = {}
        yscale = {}
        acc = {}
        hb = {}
        sums = {}
        negmu = {}
        ssq = {}
        rstd = {}
        tt = {}
        hb_ps = {}

        batch_of = {}
        quant_tick = {}
        prep_tick = {}
        last_tick = 0
        for b, (q0, n) in enumerate(BATCHES):
            for q in range(q0, q0 + n):
                batch_of[q] = (b, q - q0)
            if b > 0:
                tick = 2 * q0 - 2
                quant_tick[tick] = b
                step = max(1, (tick - last_tick) // n)
                for q in range(q0, q0 + n):
                    prep_tick[tick - 1 - step * (q0 + n - 1 - q)] = q
                last_tick = tick

        def load_y(q):
            y_t[q] = ypool.tile([P, 2 * FF], BF16, name="y_t")
            nc.sync.dma_start(out=y_t[q][:], in_=y_v[q])

        def alloc_h(q):
            h_t[q] = hpool.tile([P, 2 * E], BF16, name="h_t")

        def load_h(q, lo, hi):
            nc.sync.dma_start(out=h_t[q][:, lo * E : hi * E], in_=h_v[q][:, lo * E : hi * E])

        def transposes(q):
            words = y_t[q][:].bitcast(F32)
            xt[q] = ps_xt.tile([P, 4, P], F32, name="xt")
            for j in range(2):
                for u in range(2):
                    nc.tensor.transpose(
                        xt[q][:, 2 * j + u, :], words[:, 256 * j + u : 256 * (j + 1) : 2], ident[:]
                    )

        def copy_y(q):
            b, k = batch_of[q]
            if k == 0:
                ygrp[b] = qpool.tile([P, BATCHES[b][1] * 2 * P * 4], BF16, name="ygrp", align_bytes=64)
            nc.scalar.copy(
                out=ygrp[b][:, k * 1024 : (k + 1) * 1024].bitcast(F32).rearrange("p (j r u) -> p j r u", j=2, u=2),
                in_=xt[q][:].rearrange("p (j u) r -> p j r u", j=2, u=2),
            )

        def quant_y(b):
            width = BATCHES[b][1] * 2 * P
            ycodes[b] = qpool.tile([P, width], U32, name="ycodes", align_bytes=64)
            yscale[b] = qpool.tile([P, width], U8, name="yscale", align_bytes=64)
            nc.vector.quantize_mx(out=ycodes[b][:].bitcast(E5X4), scales=yscale[b][:], in_=ygrp[b][:])

        def mm(i):
            q, j = divmod(i, 2)
            q, k = batch_of[q]
            cols = slice((2 * k + j) * P, (2 * k + j + 1) * P)
            for n in range(NH):
                acc[(i, n)] = ps_acc.tile([P, NB], F32, name="acc%d" % n)
                nc.tensor.matmul_mx(
                    out=acc[(i, n)][:],
                    lhsT=ycodes[q][:, cols].bitcast(E5X4),
                    lhsT_scale=yscale[q][:, cols],
                    rhs=w_codes[:, n * NB : (n + 1) * NB].bitcast(E5X4),
                    rhs_scale=w_scale[:, n * NB : (n + 1) * NB],
                    start=True,
                    stop=True,
                )

        def p2(i):
            q, j = divmod(i, 2)
            hb[i] = rpool.tile([P, E], F32, name="hb")
            nc.gpsimd.tensor_tensor(out=hb[i][:], in0=h_t[q][:, j * E : (j + 1) * E], in1=b2_sb[:], op=ALU.add)

        def pe_mm(i, pool, names):
            q, j = divmod(i, 2)
            for n in range(NH):
                hb_ps[(i, n)] = pool.tile([P, NB], F32, name=names[n])
                nc.tensor.matmul(
                    out=hb_ps[(i, n)][:],
                    lhsT=ident_bf[:],
                    rhs=h_t[q][:, j * E + n * NB : j * E + (n + 1) * NB],
                    start=True,
                    stop=False,
                )
                nc.tensor.matmul(
                    out=hb_ps[(i, n)][:], lhsT=ones[:], rhs=rows[:, n * NB : (n + 1) * NB], start=False, stop=True
                )

        def pe_mm_cols(i):
            q, j = divmod(i, 2)
            for n in range(NH):
                hb_ps[(i, n)] = ps_xt.tile([P, NB], F32, name="xt")
                for c in range(4):
                    col = 4 * n + c
                    nc.tensor.matmul(
                        out=hb_ps[(i, n)][:, c * P : (c + 1) * P],
                        lhsT=b2c[:, col : col + 1].to_broadcast([P, P]),
                        rhs=ident[:],
                        is_transpose=True,
                        start=c == 0,
                        stop=False,
                    )
                nc.tensor.matmul(
                    out=hb_ps[(i, n)][:],
                    lhsT=ident_bf[:],
                    rhs=h_t[q][:, j * E + n * NB : j * E + (n + 1) * NB],
                    start=False,
                    stop=True,
                )

        def pe_copy(i, copiers):
            hb[i] = rpool.tile([P, E], F32, name="hb")
            for n in range(NH):
                copiers[n](out=hb[i][:, n * NB : (n + 1) * NB], in_=hb_ps[(i, n)][:])

        def pe_hb(i, pool, names, copiers):
            pe_mm(i, pool, names)
            pe_copy(i, copiers)

        def p1(i, n):
            if n == 0:
                sums[i] = spool.tile([P, NH], F32, name="sums")
            half = slice(n * NB, (n + 1) * NB)
            nc.vector.scalar_tensor_tensor(
                out=hb[i][:, half],
                in0=acc[(i, n)][:],
                scalar=0.0,
                in1=hb[i][:, half],
                op0=ALU.add,
                op1=ALU.add,
                accum_out=sums[i][:, n : n + 1],
            )

        def neg_mean(i):
            negmu[i] = spool.tile([P, 1], F32, name="negmu")
            nc.vector.tensor_scalar(
                out=negmu[i][:],
                in0=sums[i][:, 0:1],
                scalar1=sums[i][:, 1:2],
                scalar2=-1.0 / E,
                op0=ALU.add,
                op1=ALU.mult,
            )

        def p3(i):
            ssq[i] = spool.tile([P, 1], F32, name="ssq")
            nc.scalar.activation(
                out=junk[:], in_=hb[i][:], func=ACT.Square, bias=negmu[i][:, 0:1], scale=1.0, accum_out=ssq[i][:]
            )

        def rsqrt(i):
            rstd[i] = spool.tile([P, 1], F32, name="rstd")
            nc.scalar.activation(
                out=rstd[i][:], in_=ssq[i][:], func=ACT.Abs_reciprocal_sqrt, bias=EPS, scale=1.0 / E
            )

        def p4(i):
            tt[i] = tpool.tile([P, E], F32, name="tt")
            nc.vector.scalar_tensor_tensor(
                out=tt[i][:],
                in0=hb[i][:],
                scalar=negmu[i][:, 0:1],
                in1=g2_ps[:],
                op0=ALU.add,
                op1=ALU.mult,
            )

        def p5_scalar(i, lo, hi):
            nc.scalar.activation(out=tt[i][:, lo:hi], in_=tt[i][:, lo:hi], func=ACT.Copy, scale=rstd[i][:, 0:1])

        def p5_gpsimd(i, lo, hi):
            nc.gpsimd.tensor_scalar(
                out=tt[i][:, lo:hi],
                in0=tt[i][:, lo:hi],
                scalar1=rstd[i][:, 0:1],
                scalar2=0.0,
                op0=ALU.mult,
                op1=ALU.add,
            )

        def p5_vector(i, lo, hi):
            nc.vector.tensor_scalar(
                out=tt[i][:, lo:hi],
                in0=tt[i][:, lo:hi],
                scalar1=rstd[i][:, 0:1],
                scalar2=0.0,
                op0=ALU.mult,
                op1=ALU.add,
            )

        def store(i, lo, hi):
            q, j = divmod(i, 2)
            nc.sync.dma_start(out=o_v[q][:, j, lo:hi], in_=tt[i][:, lo:hi])

        def p5_store(i):
            if i == NT - 1:
                p5_scalar(i, 0, NB)
                store(i, 0, NB)
                p5_vector(i, NB, E)
                store(i, NB, E)
            elif i == NT - 2:
                p5_gpsimd(i, 0, NB)
                store(i, 0, NB)
                p5_scalar(i, NB, E)
                store(i, NB, E)
            elif i >= NT - 3:
                p5_gpsimd(i, 0, E)
                store(i, 0, E)
            else:
                p5_scalar(i, 0, E)
                store(i, 0, E)

        rows = const.tile([P, 2 * E], BF16, name="rows")
        ones = const.tile([P, P], BF16, name="ones")
        vec = const.tile([P, P], BF16, name="vec")
        one1 = const.tile([P, 1], F32, name="one1")
        warm = const.tile([P, 1], F32, name="warm")
        junk = const.tile([P, E], F32, name="junk")
        w_raw = const.tile([P, 4, E], BF16, name="w_raw")
        nc.vector.memset(rows[:], 0.0)
        nc.vector.memset(ones[:], 1.0)
        nc.vector.memset(vec[:], 0.0)
        nc.vector.memset(one1[:], 1.0)

        load_y(0)
        load_y(1)
        nc.sync.dma_start(out=rows[0:1, 0:E], in_=b2.rearrange("(o e) -> o e", o=1))
        nc.sync.dma_start(out=rows[0:1, E : 2 * E], in_=g2.rearrange("(o e) -> o e", o=1))
        nc.sync.dma_start(out=w_raw[:, :, 0:NB], in_=w_v[:, :, 0:NB])
        alloc_h(0)
        load_h(0, 0, 1)
        nc.sync.dma_start(out=w_raw[:, :, NB:E], in_=w_v[:, :, NB:E])
        load_h(0, 1, 2)
        nc.sync.dma_start(out=vec[0:NC, :], in_=b2.rearrange("(c e) -> c e", c=NC))
        for q in range(1, H_AHEAD):
            load_y(2 * q)
            load_y(2 * q + 1)
            alloc_h(q)
            load_h(q, 0, 2)

        nc.scalar.activation(out=warm[:], in_=one1[:], func=ACT.Abs_reciprocal_sqrt)

        ident = const.tile([P, P], F32, name="ident")
        make_identity(nc, ident[:])
        ident_bf = const.tile([P, P], BF16, name="ident_bf")
        make_identity(nc, ident_bf[:])

        transposes(0)
        copy_y(0)
        transposes(1)
        copy_y(1)

        b2_sb = const.tile([P, E], F32, name="b2_sb")
        for n in range(NH):
            b2_ps = ps_acc.tile([P, NB], F32, name="acc%d" % n)
            nc.tensor.matmul(out=b2_ps[:], lhsT=ones[:], rhs=rows[:, n * NB : (n + 1) * NB], start=True, stop=True)
            nc.scalar.copy(out=b2_sb[:, n * NB : (n + 1) * NB], in_=b2_ps[:])
        g2_ps = ps_g2.tile([P, E], BF16, name="g2_ps")
        for n in range(NH):
            nc.tensor.matmul(
                out=g2_ps[:, n * NB : (n + 1) * NB],
                lhsT=ones[:],
                rhs=rows[:, E + n * NB : E + (n + 1) * NB],
                start=True,
                stop=True,
            )

        w_grp = const.tile([P, E, 4], BF16, name="w_grp", align_bytes=64)
        w_codes = const.tile([P, E], U32, name="w_codes", align_bytes=64)
        w_scale = const.tile([P, E], U8, name="w_scale", align_bytes=64)

        def w_views(lo, hi):
            return w_grp[:, lo:hi, :], w_raw[:, :, lo:hi].rearrange("p j w -> p w j")

        def w_quant(n):
            nc.vector.quantize_mx(
                out=w_codes[:, n * NB : (n + 1) * NB].bitcast(E5X4),
                scales=w_scale[:, n * NB : (n + 1) * NB],
                in_=w_grp[:, n * NB : (n + 1) * NB, :].rearrange("p w j -> p (w j)"),
            )

        dst, src = w_views(0, NB)
        nc.vector.tensor_copy(out=dst, in_=src)
        quant_y(0)
        dst, src = w_views(NB, NB + W_V_COLS)
        nc.vector.tensor_copy(out=dst, in_=src)
        dst, src = w_views(NB + W_V_COLS, E)
        nc.scalar.copy(out=dst, in_=src)
        w_quant(0)
        w_quant(1)

        for i in PE_HEAD:
            pe_hb(i, ps_acc, ("acc0", "acc1"), (nc.scalar.copy, nc.scalar.copy))
        mm(0)
        v_ps = ps_xt.tile([P, P], BF16, name="xt")
        nc.tensor.transpose(v_ps[:], vec[:], ident_bf[:])
        b2c = const.tile([P, NC], F32, name="b2c")
        nc.scalar.copy(out=b2c[:], in_=v_ps[:, 0:NC])
        pe_tiles = list(PE_HEAD) + [PE_TICK[t] for t in PE_TICK]

        for i in range(NT + 3):
            q = i // 2
            even = i % 2 == 0
            if even and q + H_AHEAD < NQ:
                alloc_h(q + H_AHEAD)
                load_h(q + H_AHEAD, 0, 2)
            if even and q + Y_AHEAD < NQ:
                load_y(q + Y_AHEAD)
            if i + G_AHEAD < NT and i + G_AHEAD not in pe_tiles:
                p2(i + G_AHEAD)
            if i == 0:
                pe_mm(PE_TICK[0], ps_xt, ("xt", "xt"))
            if i + 1 < NT:
                mm(i + 1)
            if i in prep_tick:
                transposes(prep_tick[i])
            if i + 1 in PE_TICK:
                pe_mm_cols(PE_TICK[i + 1])
            if i < NT:
                p1(i, 0)
            if i < NT:
                p1(i, 1)
            if i == NT - 1:
                neg_mean(i)
            if 0 <= i - 1 < NT:
                p4(i - 1)
            if i < NT - 1:
                neg_mean(i)
            if i in quant_tick:
                quant_y(quant_tick[i])
            if 0 <= i - 1 < NT:
                p3(i - 1)
            if 0 <= i - 2 < NT:
                p5_store(i - 2)
            if 0 <= i - 1 < NT:
                rsqrt(i - 1)
            if i in prep_tick:
                copy_y(prep_tick[i])
            if i in PE_TICK:
                pe_copy(PE_TICK[i], (nc.vector.tensor_copy, nc.vector.tensor_copy if i == 0 else nc.scalar.copy))
